import numpy as np
import ml_dtypes


def mxq(x, axis, fmt="e4m3"):
    dtype, down = {"e4m3": (ml_dtypes.float8_e4m3fn, 7), "e5m2": (ml_dtypes.float8_e5m2, 14)}[fmt]
    v = np.moveaxis(np.asarray(x, np.float32).astype(ml_dtypes.bfloat16).astype(np.float64), axis, -1)
    blocks = v.reshape(v.shape[:-1] + (-1, 32))
    amax = np.abs(blocks).max(-1, keepdims=True)
    byte = np.maximum(np.where(amax > 0, np.frexp(amax)[1] - 1 + 127, 0) - down, 1)
    scale = np.exp2(byte - 127.0)
    codes = (blocks / scale).astype(np.float32).astype(dtype).astype(np.float64)
    return np.moveaxis((codes * scale).reshape(v.shape), -1, axis)


WIDE = False


def mx_kscale(k):
    if not WIDE:
        return np.ones(k)
    levels = np.array([10, -10, 5, -5, 0])
    a = np.random.permutation(np.resize(levels, k // 512 * 4)).reshape(k // 512, 4)
    idx = np.arange(k)
    return np.exp2(a[idx // 512, idx % 128 // 32])


BF16 = ml_dtypes.bfloat16


def bf(x):
    return np.asarray(x, np.float32).astype(BF16)


def f64(x):
    return np.asarray(x).astype(np.float64)


E2M1 = np.array([0.0, 0.5, 1.0, 1.5, 2.0, 3.0, 4.0, 6.0, -0.0, -0.5, -1.0, -1.5, -2.0, -3.0, -4.0, -6.0])


def pack_weight(w, fmt):
    k, n = w.shape
    w = f64(bf(w)).reshape(k // 32, 32, n)
    amax = np.abs(w).max(1)
    if fmt == "e4m3":
        byte = np.frexp(amax)[1] - 1 + 127 - 7
    else:
        mant, ex = np.frexp(amax / 6.0)
        byte = np.where(mant > 0.5, ex, ex - 1) + 127
    byte = np.clip(np.where(amax > 0, byte, 1), 1, 254)
    scaled = (w * np.exp2(127.0 - byte)[:, None, :]).reshape(k, n).astype(np.float32)
    by_word = np.ascontiguousarray(scaled.reshape(k // 512, 128, 4, n).transpose(0, 1, 3, 2))
    if fmt == "e4m3":
        words = by_word.astype(ml_dtypes.float8_e4m3fn).view(np.uint8)
    else:
        c = by_word.astype(ml_dtypes.float4_e2m1fn).view(np.uint8) & 0xF
        words = c[..., 0::2] | (c[..., 1::2] << 4)
    return np.ascontiguousarray(words), np.ascontiguousarray(byte.astype(np.uint8).reshape(k // 512, 16, n))


def unpack_weight(words, scales, fmt):
    g, p, n, _ = words.shape
    if fmt == "e4m3":
        vals = np.ascontiguousarray(words).view(ml_dtypes.float8_e4m3fn).astype(np.float64)
    else:
        nib = np.empty((g, p, n, 4), np.uint8)
        nib[..., 0::2] = words & 0xF
        nib[..., 1::2] = words >> 4
        vals = E2M1[nib]
    vals = vals * np.repeat(np.exp2(scales.astype(np.float64) - 127.0), 8, axis=1)[..., None]
    return vals.transpose(0, 1, 3, 2).reshape(g * 512, n)


N, E, C, D1, D2 = 1024, 2048, 512, 2, 2
T1 = D1 + 1


def shift_down(y, k):
    return np.pad(y, ((k, 0), (0, 0)))[:y.shape[0]] if k > 0 else y


def setup_inputs():
    s = mx_kscale(E)
    x = bf(np.random.standard_normal((N, E)) * s)
    W1 = np.random.standard_normal((T1, E, C)) * 0.4 / np.sqrt(E) / s[None, :, None]
    W1_words, W1_scales = pack_weight(W1.reshape(-1, C), "e4m3")
    b1 = bf(np.random.standard_normal((1, C)) * 0.25)
    return {"x": x, "W1_words": W1_words, "W1_scales": W1_scales, "b1": b1}


def reference(x, W1_words, W1_scales, b1):
    Y = mxq(f64(x), 1, "e4m3") @ unpack_weight(W1_words, W1_scales, "e4m3").reshape(T1, E, C)
    S = sum(shift_down(Y[k], k) for k in range(T1))
    cnt1 = np.minimum(np.arange(N), D1) + 1.0
    return np.tanh(S + cnt1[:, None] * f64(b1)[0])

@@ -1,0 +1,179 @@
+from contextlib import ExitStack
+
+import concourse.mybir as mybir
+from concourse.masks import make_identity
+
+F32 = mybir.dt.float32
+BF16 = mybir.dt.bfloat16
+I32 = mybir.dt.int32
+U32 = mybir.dt.uint32
+U8 = mybir.dt.uint8
+FP8X4 = mybir.dt.float8_e4m3fn_x4
+
+P = 128
+PACK = 4
+K_PASS = P * PACK
+
+ROWS, E, C, TAPS = 1024, 2048, 512, 3
+GROUPS = E // K_PASS
+SLABS = ROWS // P
+WRAP = TAPS - 1
+POSITIONS = SLABS + WRAP
+F32_WORDS = K_PASS // 2
+FIRST_TAP = TAPS - 1
+
+FLOPS = 2 * ROWS * TAPS * E * C
+
+
+def tile_predictor_pa_e_kernel(tc, x, W1_words, W1_scales, b1, out):
+    nc = tc.nc
+    x_by_slab = x.rearrange("(j s) k -> s j k", s=SLABS)
+    out_by_slab = out.rearrange("(j s) c -> s j c", s=SLABS)
+    w_words_by_group = W1_words.rearrange("g p n t -> g p (n t)")
+    w_scales_by_row = W1_scales.rearrange("g q n -> q g n")
+
+    with ExitStack() as ctx:
+        ctx.enter_context(tc.manual_schedule())
+        keep = ctx.enter_context(tc.tile_pool(name="keep", bufs=1))
+        stage = ctx.enter_context(tc.tile_pool(name="stage", bufs=3))
+        psum = ctx.enter_context(tc.psum_pool(name="psum", bufs=8))
+
+        x_sb = [keep.tile([P, E], BF16, name="x_sb%d" % s) for s in range(SLABS)]
+        x_codes = [
+            keep.tile([P, GROUPS * P], U32, name="x_codes%d" % c, align_bytes=64)
+            for c in range(POSITIONS)
+        ]
+        x_scales = [
+            keep.tile([P, GROUPS * P], U8, name="x_scales%d" % c, align_bytes=64)
+            for c in range(POSITIONS)
+        ]
+        w_codes = [
+            keep.tile([P, C], U32, name="w_codes%d" % g, align_bytes=64)
+            for g in range(TAPS * GROUPS)
+        ]
+        w_scales = keep.tile([P, TAPS * GROUPS, C], U8, align_bytes=64)
+        identity = keep.tile([P, P], F32)
+        shift = keep.tile([P, P], F32)
+        ones = keep.tile([P, P], BF16)
+        b_row = keep.tile([P, C], BF16)
+        bias = keep.tile([P, C], F32)
+        counts = keep.tile([P, SLABS], F32)
+
+        nc.vector.memset(b_row[:], 0.0)
+        nc.scalar.dma_start(out=b_row[0:1, :], in_=b1)
+        nc.vector.memset(w_scales[:].bitcast(I32), 0)
+        nc.vector.memset(ones[:], 1.0)
+        make_identity(nc, identity[:])
+        nc.vector.memset(shift[:], 0.0)
+        nc.vector.tensor_copy(out=shift[:, 1:P], in_=identity[:, 0 : P - 1])
+        nc.vector.memset(counts[:], float(TAPS))
+        for row in range(WRAP):
+            nc.vector.memset(counts[0:1, row : row + 1], float(row + 1))
+
+        def load_x(s):
+            nc.sync.dma_start(out=x_sb[s][:], in_=x_by_slab[s])
+
+        def load_w_scales():
+            for low in range(2 * PACK):
+                quadrant, r = divmod(low, PACK)
+                nc.sync.dma_start(
+                    out=w_scales[32 * quadrant + r : P : 64].bitcast(I32),
+                    in_=w_scales_by_row[low : 16 : 2 * PACK].bitcast(I32),
+                )
+
+        def load_w_codes(tap):
+            for g in range(GROUPS * tap, GROUPS * (tap + 1)):
+                nc.sync.dma_start(out=w_codes[g][:].bitcast(I32), in_=w_words_by_group[g].bitcast(I32))
+
+        slab_order = list(range(SLABS - WRAP, SLABS)) + list(range(SLABS - WRAP))
+        for s in slab_order[:WRAP]:
+            load_x(s)
+        load_w_scales()
+        for s in slab_order[WRAP:]:
+            load_x(s)
+        for tap in reversed(range(TAPS)):
+            load_w_codes(tap)
+
+        bias_bank = psum.tile([P, C], F32, tag="bank")
+        nc.tensor.matmul(out=bias_bank[:], lhsT=ones[:], rhs=b_row[:], start=True, stop=True)
+        nc.vector.tensor_copy(out=bias[:], in_=bias_bank[:])
+
+        def transpose_position(c, turn):
+            words = x_sb[(c - WRAP) % SLABS][:].bitcast(F32)
+            permutation = shift if c < WRAP else identity
+            grouped = stage.tile([P, GROUPS, P, PACK], BF16, align_bytes=64)
+            for half in range(GROUPS // 2):
+                bank = psum.tile([P, 2, 2, P], F32, tag="bank")
+                for g in range(2):
+                    for u in range(2):
+                        group = 2 * half + g
+                        nc.tensor.transpose(
+                            bank[:, g, u, :],
+                            words[:, F32_WORDS * group + u : F32_WORDS * (group + 1) : 2],
+                            permutation[:],
+                        )
+                dst = grouped[:, 2 * half : 2 * half + 2].bitcast(F32)
+                src = bank[:].rearrange("p g u j -> p g j u")
+                if half == 1 and turn % 2 == 1:
+                    nc.vector.tensor_copy(out=dst, in_=src)
+                else:
+                    nc.scalar.copy(out=dst, in_=src)
+            return grouped
+
+        def quantise_position(c, grouped):
+            nc.vector.quantize_mx(
+                out=x_codes[c][:].bitcast(FP8X4),
+                scales=x_scales[c][:],
+                in_=grouped[:].rearrange("p g j t -> p (g j t)"),
+            )
+
+        position_order = []
+        for s in slab_order:
+            if s >= SLABS - WRAP:
+                position_order.append(s + WRAP - SLABS)
+            position_order.append(s + WRAP)
+
+        waiting = None
+        for turn, c in enumerate(position_order):
+            grouped = transpose_position(c, turn)
+            if waiting is not None:
+                quantise_position(*waiting)
+            waiting = (c, grouped)
+        quantise_position(*waiting)
+
+        acc = [psum.tile([P, C], F32, tag="bank", name="acc%d" % s) for s in range(SLABS)]
+
+        def mx_pass(s, tap, g, start, stop):
+            c = s + WRAP - tap
+            cols = slice(P * g, P * (g + 1))
+            w_group = GROUPS * tap + g
+            nc.tensor.matmul_mx(
+                out=acc[s][:],
+                lhsT=x_codes[c][:, cols].bitcast(FP8X4),
+                lhsT_scale=x_scales[c][:, cols],
+                rhs=w_codes[w_group][:].bitcast(FP8X4),
+                rhs_scale=w_scales[:, w_group, :],
+                start=start,
+                stop=stop,
+            )
+
+        for g in range(GROUPS):
+            for s in range(SLABS):
+                mx_pass(s, FIRST_TAP, g, start=(g == 0), stop=False)
+
+        for s in range(SLABS):
+            for tap in reversed(range(FIRST_TAP)):
+                for g in range(GROUPS):
+                    mx_pass(s, tap, g, start=False, stop=(tap == 0 and g == GROUPS - 1))
+            biased = stage.tile([P, C], F32)
+            nc.vector.scalar_tensor_tensor(
+                out=biased[:],
+                in0=bias[:],
+                scalar=counts[:, s : s + 1],
+                in1=acc[s][:],
+                op0=mybir.AluOpType.mult,
+                op1=mybir.AluOpType.add,
+            )
+            result = stage.tile([P, C], F32)
+            nc.scalar.activation(out=result[:], in_=biased[:], func=mybir.ActivationFunctionType.Tanh)
+            nc.sync.dma_start(out=out_by_slab[s], in_=result[:])

@@ -30,7 +30,6 @@ def tile_predictor_pa_e_kernel(tc, x, W1_words, W1_scales, b1, out):
     x_by_slab = x.rearrange("(j s) k -> s j k", s=SLABS)
     out_by_slab = out.rearrange("(j s) c -> s j c", s=SLABS)
     w_words_by_group = W1_words.rearrange("g p n t -> g p (n t)")
-    w_scales_by_row = W1_scales.rearrange("g q n -> q g n")
 
     with ExitStack() as ctx:
         ctx.enter_context(tc.manual_schedule())
@@ -51,18 +50,13 @@ def tile_predictor_pa_e_kernel(tc, x, W1_words, W1_scales, b1, out):
             keep.tile([P, C], U32, name="w_codes%d" % g, align_bytes=64)
             for g in range(TAPS * GROUPS)
         ]
-        w_scales = keep.tile([P, TAPS * GROUPS, C], U8, align_bytes=64)
+        w_scales = keep.tile([P, TAPS, C], U8, align_bytes=64)
         identity = keep.tile([P, P], F32)
         shift = keep.tile([P, P], F32)
-        ones = keep.tile([P, P], BF16)
-        b_row = keep.tile([P, C], BF16)
-        bias = keep.tile([P, C], F32)
+        bias = keep.tile([P, C], BF16)
         counts = keep.tile([P, SLABS], F32)
 
-        nc.vector.memset(b_row[:], 0.0)
-        nc.scalar.dma_start(out=b_row[0:1, :], in_=b1)
         nc.vector.memset(w_scales[:].bitcast(I32), 0)
-        nc.vector.memset(ones[:], 1.0)
         make_identity(nc, identity[:])
         nc.vector.memset(shift[:], 0.0)
         nc.vector.tensor_copy(out=shift[:, 1:P], in_=identity[:, 0 : P - 1])
@@ -70,15 +64,18 @@ def tile_predictor_pa_e_kernel(tc, x, W1_words, W1_scales, b1, out):
         for row in range(WRAP):
             nc.vector.memset(counts[0:1, row : row + 1], float(row + 1))
 
-        def load_x(s):
-            nc.sync.dma_start(out=x_sb[s][:], in_=x_by_slab[s])
+        def load_x(s, pieces):
+            width = E // pieces
+            for piece in range(pieces):
+                cols = slice(width * piece, width * (piece + 1))
+                nc.sync.dma_start(out=x_sb[s][:, cols], in_=x_by_slab[s][:, cols])
 
-        def load_w_scales():
-            for low in range(2 * PACK):
-                quadrant, r = divmod(low, PACK)
+        def load_w_scales(tap):
+            groups = slice(GROUPS * tap, GROUPS * (tap + 1))
+            for quadrant in range(4):
                 nc.sync.dma_start(
-                    out=w_scales[32 * quadrant + r : P : 64].bitcast(I32),
-                    in_=w_scales_by_row[low : 16 : 2 * PACK].bitcast(I32),
+                    out=w_scales[32 * quadrant : 32 * quadrant + 16, tap, :].bitcast(I32),
+                    in_=W1_scales[groups, 4 * quadrant : 4 * quadrant + 4, :].bitcast(I32),
                 )
 
         def load_w_codes(tap):
@@ -86,17 +83,14 @@ def tile_predictor_pa_e_kernel(tc, x, W1_words, W1_scales, b1, out):
                 nc.sync.dma_start(out=w_codes[g][:].bitcast(I32), in_=w_words_by_group[g].bitcast(I32))
 
         slab_order = list(range(SLABS - WRAP, SLABS)) + list(range(SLABS - WRAP))
-        for s in slab_order[:WRAP]:
-            load_x(s)
-        load_w_scales()
-        for s in slab_order[WRAP:]:
-            load_x(s)
-        for tap in reversed(range(TAPS)):
+        tap_order = list(reversed(range(TAPS)))
+        for n, s in enumerate(slab_order):
+            load_x(s, pieces=(GROUPS if n == 0 else 1))
+            if n % 2 == 1 and n // 2 < TAPS:
+                load_w_scales(tap_order[n // 2])
+        for tap in tap_order:
             load_w_codes(tap)
-
-        bias_bank = psum.tile([P, C], F32, tag="bank")
-        nc.tensor.matmul(out=bias_bank[:], lhsT=ones[:], rhs=b_row[:], start=True, stop=True)
-        nc.vector.tensor_copy(out=bias[:], in_=bias_bank[:])
+        nc.sync.dma_start(out=bias[:], in_=b1[0].partition_broadcast(P))
 
         def transpose_position(c, turn):
             words = x_sb[(c - WRAP) % SLABS][:].bitcast(F32)
@@ -152,7 +146,7 @@ def tile_predictor_pa_e_kernel(tc, x, W1_words, W1_scales, b1, out):
                 lhsT=x_codes[c][:, cols].bitcast(FP8X4),
                 lhsT_scale=x_scales[c][:, cols],
                 rhs=w_codes[w_group][:].bitcast(FP8X4),
-                rhs_scale=w_scales[:, w_group, :],
+                rhs_scale=w_scales[PACK * g : P, tap, :],
                 start=start,
                 stop=stop,
             )
@@ -166,14 +160,18 @@ def tile_predictor_pa_e_kernel(tc, x, W1_words, W1_scales, b1, out):
                 for g in range(GROUPS):
                     mx_pass(s, tap, g, start=False, stop=(tap == 0 and g == GROUPS - 1))
             biased = stage.tile([P, C], F32)
-            nc.vector.scalar_tensor_tensor(
-                out=biased[:],
-                in0=bias[:],
-                scalar=counts[:, s : s + 1],
-                in1=acc[s][:],
-                op0=mybir.AluOpType.mult,
-                op1=mybir.AluOpType.add,
-            )
             result = stage.tile([P, C], F32)
-            nc.scalar.activation(out=result[:], in_=biased[:], func=mybir.ActivationFunctionType.Tanh)
-            nc.sync.dma_start(out=out_by_slab[s], in_=result[:])
+            for half in range(2):
+                cols = slice(C // 2 * half, C // 2 * (half + 1))
+                nc.vector.scalar_tensor_tensor(
+                    out=biased[:, cols],
+                    in0=bias[:, cols],
+                    scalar=counts[:, s : s + 1],
+                    in1=acc[s][:, cols],
+                    op0=mybir.AluOpType.mult,
+                    op1=mybir.AluOpType.add,
+                )
+                nc.scalar.activation(
+                    out=result[:, cols], in_=biased[:, cols], func=mybir.ActivationFunctionType.Tanh
+                )
+                nc.sync.dma_start(out=out_by_slab[s][:, cols], in_=result[:, cols])

@@ -20,7 +20,6 @@ SLABS = ROWS // P
 WRAP = TAPS - 1
 POSITIONS = SLABS + WRAP
 F32_WORDS = K_PASS // 2
-FIRST_TAP = TAPS - 1
 
 FLOPS = 2 * ROWS * TAPS * E * C
 
@@ -52,14 +51,11 @@ def tile_predictor_pa_e_kernel(tc, x, W1_words, W1_scales, b1, out):
         ]
         w_scales = keep.tile([P, TAPS, C], U8, align_bytes=64)
         identity = keep.tile([P, P], F32)
-        shift = keep.tile([P, P], F32)
         bias = keep.tile([P, C], BF16)
         counts = keep.tile([P, SLABS], F32)
 
         nc.vector.memset(w_scales[:].bitcast(I32), 0)
         make_identity(nc, identity[:])
-        nc.vector.memset(shift[:], 0.0)
-        nc.vector.tensor_copy(out=shift[:, 1:P], in_=identity[:, 0 : P - 1])
         nc.vector.memset(counts[:], float(TAPS))
         for row in range(WRAP):
             nc.vector.memset(counts[0:1, row : row + 1], float(row + 1))
@@ -82,19 +78,18 @@ def tile_predictor_pa_e_kernel(tc, x, W1_words, W1_scales, b1, out):
             for g in range(GROUPS * tap, GROUPS * (tap + 1)):
                 nc.sync.dma_start(out=w_codes[g][:].bitcast(I32), in_=w_words_by_group[g].bitcast(I32))
 
-        slab_order = list(range(SLABS - WRAP, SLABS)) + list(range(SLABS - WRAP))
-        tap_order = list(reversed(range(TAPS)))
-        for n, s in enumerate(slab_order):
-            load_x(s, pieces=(GROUPS if n == 0 else 1))
-            if n % 2 == 1 and n // 2 < TAPS:
-                load_w_scales(tap_order[n // 2])
-        for tap in tap_order:
+        for s in range(SLABS):
+            load_x(s, pieces=(GROUPS if s in (0, SLABS - 1) else 1))
+            if s == 1:
+                load_w_scales(0)
+        load_w_codes(0)
+        for tap in range(1, TAPS):
+            load_w_scales(tap)
             load_w_codes(tap)
         nc.sync.dma_start(out=bias[:], in_=b1[0].partition_broadcast(P))
 
-        def transpose_position(c, turn):
-            words = x_sb[(c - WRAP) % SLABS][:].bitcast(F32)
-            permutation = shift if c < WRAP else identity
+        def transpose_slab(s):
+            words = x_sb[s][:].bitcast(F32)
             grouped = stage.tile([P, GROUPS, P, PACK], BF16, align_bytes=64)
             for half in range(GROUPS // 2):
                 bank = psum.tile([P, 2, 2, P], F32, tag="bank")
@@ -104,11 +99,11 @@ def tile_predictor_pa_e_kernel(tc, x, W1_words, W1_scales, b1, out):
                         nc.tensor.transpose(
                             bank[:, g, u, :],
                             words[:, F32_WORDS * group + u : F32_WORDS * (group + 1) : 2],
-                            permutation[:],
+                            identity[:],
                         )
                 dst = grouped[:, 2 * half : 2 * half + 2].bitcast(F32)
                 src = bank[:].rearrange("p g u j -> p g j u")
-                if half == 1 and turn % 2 == 1:
+                if half == 1 and s % 2 == 1:
                     nc.vector.tensor_copy(out=dst, in_=src)
                 else:
                     nc.scalar.copy(out=dst, in_=src)
@@ -121,19 +116,23 @@ def tile_predictor_pa_e_kernel(tc, x, W1_words, W1_scales, b1, out):
                 in_=grouped[:].rearrange("p g j t -> p (g j t)"),
             )
 
-        position_order = []
-        for s in slab_order:
-            if s >= SLABS - WRAP:
-                position_order.append(s + WRAP - SLABS)
-            position_order.append(s + WRAP)
+        def move_on_one_column(grouped):
+            moved = stage.tile([P, GROUPS, P, PACK], BF16, align_bytes=64)
+            nc.vector.memset(moved[:, :, 0, :].bitcast(F32), 0.0)
+            nc.vector.tensor_copy(
+                out=moved[:, :, 1:P, :].bitcast(F32), in_=grouped[:, :, 0 : P - 1, :].bitcast(F32)
+            )
+            return moved
 
-        waiting = None
-        for turn, c in enumerate(position_order):
-            grouped = transpose_position(c, turn)
-            if waiting is not None:
-                quantise_position(*waiting)
-            waiting = (c, grouped)
-        quantise_position(*waiting)
+        grouped_of = [transpose_slab(0)]
+        for s in range(1, SLABS):
+            grouped_of.append(transpose_slab(s))
+            quantise_position(s - 1 + WRAP, grouped_of[s - 1])
+        quantise_position(SLABS - 1 + WRAP, grouped_of[SLABS - 1])
+
+        moved_of = [move_on_one_column(grouped_of[SLABS - WRAP + c]) for c in range(WRAP)]
+        for c in range(WRAP):
+            quantise_position(c, moved_of[c])
 
         acc = [psum.tile([P, C], F32, tag="bank", name="acc%d" % s) for s in range(SLABS)]
 
@@ -153,12 +152,12 @@ def tile_predictor_pa_e_kernel(tc, x, W1_words, W1_scales, b1, out):
 
         for g in range(GROUPS):
             for s in range(SLABS):
-                mx_pass(s, FIRST_TAP, g, start=(g == 0), stop=False)
+                mx_pass(s, 0, g, start=(g == 0), stop=False)
 
         for s in range(SLABS):
-            for tap in reversed(range(FIRST_TAP)):
+            for tap in range(1, TAPS):
                 for g in range(GROUPS):
-                    mx_pass(s, tap, g, start=False, stop=(tap == 0 and g == GROUPS - 1))
+                    mx_pass(s, tap, g, start=False, stop=(tap == TAPS - 1 and g == GROUPS - 1))
             biased = stage.tile([P, C], F32)
             result = stage.tile([P, C], F32)
             for half in range(2):

@@ -27,16 +27,33 @@ FLOPS = 2 * ROWS * TAPS * E * C
 def tile_predictor_pa_e_kernel(tc, x, W1_words, W1_scales, b1, out):
     nc = tc.nc
     x_by_slab = x.rearrange("(j s) k -> s j k", s=SLABS)
+    x_by_block = x.rearrange("(b beta s) k -> b beta (s k)", s=SLABS, beta=32).rearrange(
+        "b beta (m a w) -> b a beta m w", a=4, w=P
+    )
     out_by_slab = out.rearrange("(j s) c -> s j c", s=SLABS)
     w_words_by_group = W1_words.rearrange("g p n t -> g p (n t)")
+    HALF = C // 2
+    ON_TENSOR = (6, 7, 0, 1)
+    PAIRS = (2, 4)
+    SPLIT = 5
 
     with ExitStack() as ctx:
         ctx.enter_context(tc.manual_schedule())
         keep = ctx.enter_context(tc.tile_pool(name="keep", bufs=1))
-        stage = ctx.enter_context(tc.tile_pool(name="stage", bufs=3))
-        psum = ctx.enter_context(tc.psum_pool(name="psum", bufs=8))
+        stage = ctx.enter_context(tc.tile_pool(name="stage", bufs=4))
+        psum = ctx.enter_context(tc.psum_pool(name="psum", bufs=1))
 
-        x_sb = [keep.tile([P, E], BF16, name="x_sb%d" % s) for s in range(SLABS)]
+        def bank_tile(b, shape, name):
+            return psum.tile(shape, F32, tag="bank%d" % b, name=name)
+
+        x_sb = {}
+        for s in ON_TENSOR:
+            x_sb[s] = keep.tile([P, E], BF16, name="x_sb%d" % s)
+        x_pair = {}
+        grouped_pair = {}
+        for s in PAIRS:
+            x_pair[s] = keep.tile([P, 4, 2 * K_PASS], BF16, name="x_pair%d" % s)
+            grouped_pair[s] = keep.tile([P, 2, GROUPS, P, PACK], BF16, name="grouped_pair%d" % s, align_bytes=64)
         x_codes = [
             keep.tile([P, GROUPS * P], U32, name="x_codes%d" % c, align_bytes=64)
             for c in range(POSITIONS)
@@ -66,33 +83,47 @@ def tile_predictor_pa_e_kernel(tc, x, W1_words, W1_scales, b1, out):
                 cols = slice(width * piece, width * (piece + 1))
                 nc.sync.dma_start(out=x_sb[s][:, cols], in_=x_by_slab[s][:, cols])
 
-        def load_w_scales(tap):
+        def load_pair(s):
+            for b in range(4):
+                for a in range(4):
+                    nc.sync.dma_start(
+                        out=x_pair[s][32 * a : 32 * a + 32, b, :].rearrange("p (m w) -> p m w", m=2 * GROUPS),
+                        in_=x_by_block[b][a][:, GROUPS * s : GROUPS * (s + 2), :],
+                    )
+
+        def load_w(tap):
             groups = slice(GROUPS * tap, GROUPS * (tap + 1))
             for quadrant in range(4):
                 nc.sync.dma_start(
                     out=w_scales[32 * quadrant : 32 * quadrant + 16, tap, :].bitcast(I32),
                     in_=W1_scales[groups, 4 * quadrant : 4 * quadrant + 4, :].bitcast(I32),
                 )
-
-        def load_w_codes(tap):
             for g in range(GROUPS * tap, GROUPS * (tap + 1)):
                 nc.sync.dma_start(out=w_codes[g][:].bitcast(I32), in_=w_words_by_group[g].bitcast(I32))
 
-        for s in range(SLABS):
-            load_x(s, pieces=(GROUPS if s in (0, SLABS - 1) else 1))
-            if s == 1:
-                load_w_scales(0)
-        load_w_codes(0)
-        for tap in range(1, TAPS):
-            load_w_scales(tap)
-            load_w_codes(tap)
+        load_x(ON_TENSOR[0], GROUPS)
+        for s in ON_TENSOR[1:]:
+            load_x(s, 1)
+        load_w(0)
+        load_w(1)
+        load_pair(PAIRS[0])
+        load_w(2)
         nc.sync.dma_start(out=bias[:], in_=b1[0].partition_broadcast(P))
+        load_pair(PAIRS[1])
 
-        def transpose_slab(s):
+        grouped_of = {}
+
+        def new_grouped(s):
+            grouped_of[s] = stage.tile(
+                [P, GROUPS, P, PACK], BF16, align_bytes=64, name="grouped%d" % s, tag="grouped"
+            )
+            return grouped_of[s]
+
+        def transpose_slab(i, s):
             words = x_sb[s][:].bitcast(F32)
-            grouped = stage.tile([P, GROUPS, P, PACK], BF16, align_bytes=64)
+            grouped = new_grouped(s)
             for half in range(GROUPS // 2):
-                bank = psum.tile([P, 2, 2, P], F32, tag="bank")
+                bank = bank_tile(2 * (i % 2) + half, [P, 2, 2, P], "turned%d_%d" % (s, half))
                 for g in range(2):
                     for u in range(2):
                         group = 2 * half + g
@@ -103,74 +134,192 @@ def tile_predictor_pa_e_kernel(tc, x, W1_words, W1_scales, b1, out):
                         )
                 dst = grouped[:, 2 * half : 2 * half + 2].bitcast(F32)
                 src = bank[:].rearrange("p g u j -> p g j u")
-                if half == 1 and s % 2 == 1:
+                if half == 1 and i % 2 == 1:
                     nc.vector.tensor_copy(out=dst, in_=src)
                 else:
                     nc.scalar.copy(out=dst, in_=src)
-            return grouped
 
         def quantise_position(c, grouped):
             nc.vector.quantize_mx(
                 out=x_codes[c][:].bitcast(FP8X4),
                 scales=x_scales[c][:],
-                in_=grouped[:].rearrange("p g j t -> p (g j t)"),
+                in_=grouped.rearrange("p g j t -> p (g j t)"),
             )
 
-        def move_on_one_column(grouped):
-            moved = stage.tile([P, GROUPS, P, PACK], BF16, align_bytes=64)
+        def move_on_one_column(grouped, name):
+            moved = stage.tile([P, GROUPS, P, PACK], BF16, align_bytes=64, name=name, tag="moved")
             nc.vector.memset(moved[:, :, 0, :].bitcast(F32), 0.0)
             nc.vector.tensor_copy(
                 out=moved[:, :, 1:P, :].bitcast(F32), in_=grouped[:, :, 0 : P - 1, :].bitcast(F32)
             )
-            return moved
+            return moved[:]
 
-        grouped_of = [transpose_slab(0)]
-        for s in range(1, SLABS):
-            grouped_of.append(transpose_slab(s))
-            quantise_position(s - 1 + WRAP, grouped_of[s - 1])
-        quantise_position(SLABS - 1 + WRAP, grouped_of[SLABS - 1])
+        sorted_of = {}
+        turned_of = {}
+        QUARTER = 2 * F32_WORDS
 
-        moved_of = [move_on_one_column(grouped_of[SLABS - WRAP + c]) for c in range(WRAP)]
-        for c in range(WRAP):
-            quantise_position(c, moved_of[c])
-
-        acc = [psum.tile([P, C], F32, tag="bank", name="acc%d" % s) for s in range(SLABS)]
-
-        def mx_pass(s, tap, g, start, stop):
-            c = s + WRAP - tap
-            cols = slice(P * g, P * (g + 1))
-            w_group = GROUPS * tap + g
-            nc.tensor.matmul_mx(
-                out=acc[s][:],
-                lhsT=x_codes[c][:, cols].bitcast(FP8X4),
-                lhsT_scale=x_scales[c][:, cols],
-                rhs=w_codes[w_group][:].bitcast(FP8X4),
-                rhs_scale=w_scales[PACK * g : P, tap, :],
-                start=start,
-                stop=stop,
+        def sort_words(s, b):
+            sorted_of[(s, b)] = stage.tile([P, QUARTER], F32, align_bytes=64, name="sorted%d_%d" % (s, b), tag="sorted")
+            nc.scalar.copy(
+                out=sorted_of[(s, b)][:].rearrange("p (u m i) -> p u m i", u=2, i=32),
+                in_=x_pair[s][:, b, :].bitcast(F32).rearrange("p (m i u) -> p u m i", u=2, i=32),
             )
 
-        for g in range(GROUPS):
-            for s in range(SLABS):
-                mx_pass(s, 0, g, start=(g == 0), stop=False)
+        def turn_blocks(s, b):
+            turned_of[(s, b)] = stage.tile([P, QUARTER], F32, align_bytes=64, name="turnedv%d_%d" % (s, b), tag="turnedv")
+            nc.vector.transpose(out=turned_of[(s, b)][:], in_=sorted_of[(s, b)][:])
 
-        for s in range(SLABS):
-            for tap in range(1, TAPS):
-                for g in range(GROUPS):
-                    mx_pass(s, tap, g, start=False, stop=(tap == TAPS - 1 and g == GROUPS - 1))
-            biased = stage.tile([P, C], F32)
-            result = stage.tile([P, C], F32)
-            for half in range(2):
-                cols = slice(C // 2 * half, C // 2 * (half + 1))
-                nc.vector.scalar_tensor_tensor(
-                    out=biased[:, cols],
-                    in0=bias[:, cols],
-                    scalar=counts[:, s : s + 1],
-                    in1=acc[s][:, cols],
-                    op0=mybir.AluOpType.mult,
-                    op1=mybir.AluOpType.add,
-                )
-                nc.scalar.activation(
-                    out=result[:, cols], in_=biased[:, cols], func=mybir.ActivationFunctionType.Tanh
-                )
-                nc.sync.dma_start(out=out_by_slab[s][:, cols], in_=result[:, cols])
+        def pair_words(s, b):
+            nc.scalar.copy(
+                out=grouped_pair[s][:].bitcast(F32).rearrange("p s g j u -> p (s g) j u")[:, :, 32 * b : 32 * (b + 1), :],
+                in_=turned_of[(s, b)][:].rearrange("p (u m beta) -> p m beta u", u=2, beta=32),
+            )
+
+        def quantise_of_pair(s, k):
+            quantise_position(s + k + WRAP, grouped_pair[s][:, k])
+
+        halves = [slice(HALF * h, HALF * (h + 1)) for h in range(2)]
+        whole = slice(0, C)
+        parts_of = {}
+        passes_done = {}
+
+        def open_slab(o, banks):
+            if len(banks) == 1:
+                parts_of[o] = [(bank_tile(banks[0], [P, C], "acc%d" % o), whole)]
+            else:
+                parts_of[o] = [
+                    (bank_tile(banks[h], [P, HALF], "acc%d_%d" % (o, h)), halves[h]) for h in range(2)
+                ]
+            for i in range(len(banks)):
+                passes_done[(o, i)] = 0
+
+        def mx_pass(o, i, tap, g):
+            acc_tile, n_cols = parts_of[o][i]
+            c = o + WRAP - tap
+            cols = slice(P * g, P * (g + 1))
+            done = passes_done[(o, i)]
+            nc.tensor.matmul_mx(
+                out=acc_tile[:],
+                lhsT=x_codes[c][:, cols].bitcast(FP8X4),
+                lhsT_scale=x_scales[c][:, cols],
+                rhs=w_codes[GROUPS * tap + g][:, n_cols].bitcast(FP8X4),
+                rhs_scale=w_scales[PACK * g : P, tap, n_cols],
+                start=(done == 0),
+                stop=(done == TAPS * GROUPS - 1),
+            )
+            passes_done[(o, i)] = done + 1
+
+        def sweep(tap, outs):
+            for g in range(GROUPS):
+                for o in outs:
+                    mx_pass(o, 0, tap, g)
+
+        def pair(o, tap, i=0):
+            for g in range(GROUPS):
+                mx_pass(o, i, tap, g)
+
+        biased_of = {}
+
+        def add_bias(o, i=0):
+            acc_tile, n_cols = parts_of[o][i]
+            biased = stage.tile([P, C], F32, name="biased%d_%d" % (o, i), tag="biased")
+            width = n_cols.stop - n_cols.start
+            nc.vector.scalar_tensor_tensor(
+                out=biased[:, 0:width],
+                in0=bias[:, n_cols],
+                scalar=counts[:, o : o + 1],
+                in1=acc_tile[:],
+                op0=mybir.AluOpType.mult,
+                op1=mybir.AluOpType.add,
+            )
+            biased_of[(o, i)] = biased
+
+        def tanh_store(o, i=0):
+            n_cols = parts_of[o][i][1]
+            width = n_cols.stop - n_cols.start
+            result = stage.tile([P, C], F32, name="result%d_%d" % (o, i), tag="result")
+            nc.scalar.activation(
+                out=result[:, 0:width], in_=biased_of[(o, i)][:, 0:width], func=mybir.ActivationFunctionType.Tanh
+            )
+            nc.sync.dma_start(out=out_by_slab[o][:, n_cols], in_=result[:, 0:width])
+
+        for i in range(len(ON_TENSOR)):
+            transpose_slab(i, ON_TENSOR[i])
+            if i > 0:
+                quantise_position(ON_TENSOR[i - 1] + WRAP, grouped_of[ON_TENSOR[i - 1]][:])
+        quantise_position(ON_TENSOR[-1] + WRAP, grouped_of[ON_TENSOR[-1]][:])
+        for c in (1, 0):
+            quantise_position(c, move_on_one_column(grouped_of[SLABS - WRAP + c], "moved%d" % c))
+
+        open_slab(6, [4])
+        open_slab(7, [5])
+        open_slab(0, [6])
+        open_slab(1, [7])
+        sweep(0, (6, 7))
+        sweep(0, (0, 1))
+        open_slab(2, [0])
+        open_slab(3, [1])
+        sweep(1, (7, 1, 2, 0))
+
+        s = PAIRS[0]
+        sort_words(s, 0)
+        for b in range(1, 4):
+            turn_blocks(s, b - 1)
+            sort_words(s, b)
+            pair_words(s, b - 1)
+        turn_blocks(s, 3)
+        pair_words(s, 3)
+        quantise_of_pair(s, 0)
+        quantise_of_pair(s, 1)
+
+        sweep(2, (2, 3, 1, 0))
+
+        s = PAIRS[1]
+        sort_words(s, 0)
+        turn_blocks(s, 0)
+        sort_words(s, 1)
+        pair_words(s, 0)
+        turn_blocks(s, 1)
+        add_bias(1)
+        sort_words(s, 2)
+        pair_words(s, 1)
+        turn_blocks(s, 2)
+        add_bias(0)
+        sort_words(s, 3)
+        pair_words(s, 2)
+        turn_blocks(s, 3)
+        pair_words(s, 3)
+        quantise_of_pair(s, 0)
+        quantise_of_pair(s, 1)
+        tanh_store(1)
+        tanh_store(0)
+
+        pair(2, 0)
+        pair(3, 1)
+        open_slab(4, [2])
+        pair(4, 2)
+        add_bias(2)
+        tanh_store(2)
+        pair(3, 0)
+        pair(4, 1)
+        open_slab(SPLIT, [3, 7])
+        pair(SPLIT, 2, 0)
+        pair(SPLIT, 2, 1)
+        add_bias(3)
+        tanh_store(3)
+        pair(4, 0)
+        pair(SPLIT, 1, 0)
+        pair(SPLIT, 1, 1)
+        pair(6, 2)
+        add_bias(4)
+        tanh_store(4)
+        pair(7, 2)
+        add_bias(7)
+        tanh_store(7)
+        pair(6, 1)
+        add_bias(6)
+        tanh_store(6)
+        for i in range(2):
+            pair(SPLIT, 0, i)
+            add_bias(SPLIT, i)
+            tanh_store(SPLIT, i)

@@ -33,8 +33,8 @@ def tile_predictor_pa_e_kernel(tc, x, W1_words, W1_scales, b1, out):
     out_by_slab = out.rearrange("(j s) c -> s j c", s=SLABS)
     w_words_by_group = W1_words.rearrange("g p n t -> g p (n t)")
     HALF = C // 2
-    ON_TENSOR = (6, 7, 0, 1)
-    PAIRS = (2, 4)
+    ON_TENSOR = (6, 7, 0, 1, 2, 3)
+    PAIRS = (4,)
     SPLIT = 5
 
     with ExitStack() as ctx:
@@ -106,17 +106,14 @@ def tile_predictor_pa_e_kernel(tc, x, W1_words, W1_scales, b1, out):
             load_x(s, 1)
         load_w(0)
         load_w(1)
-        load_pair(PAIRS[0])
         load_w(2)
         nc.sync.dma_start(out=bias[:], in_=b1[0].partition_broadcast(P))
-        load_pair(PAIRS[1])
+        load_pair(PAIRS[0])
 
         grouped_of = {}
 
         def new_grouped(s):
-            grouped_of[s] = stage.tile(
-                [P, GROUPS, P, PACK], BF16, align_bytes=64, name="grouped%d" % s, tag="grouped"
-            )
+            grouped_of[s] = keep.tile([P, GROUPS, P, PACK], BF16, align_bytes=64, name="grouped%d" % s)
             return grouped_of[s]
 
         def transpose_slab(i, s):
@@ -255,64 +252,37 @@ def tile_predictor_pa_e_kernel(tc, x, W1_words, W1_scales, b1, out):
         open_slab(7, [5])
         open_slab(0, [6])
         open_slab(1, [7])
-        sweep(0, (6, 7))
-        sweep(0, (0, 1))
         open_slab(2, [0])
         open_slab(3, [1])
-        sweep(1, (7, 1, 2, 0))
+        sweep(0, (6, 7, 0, 1, 2, 3))
 
         s = PAIRS[0]
         sort_words(s, 0)
-        for b in range(1, 4):
-            turn_blocks(s, b - 1)
-            sort_words(s, b)
-            pair_words(s, b - 1)
-        turn_blocks(s, 3)
-        pair_words(s, 3)
+        for o in range(4):
+            pair(o, 1)
+            pair(o, 2)
+            add_bias(o)
+            turn_blocks(s, o)
+            tanh_store(o)
+            if o < 3:
+                sort_words(s, o + 1)
+            pair_words(s, o)
         quantise_of_pair(s, 0)
         quantise_of_pair(s, 1)
 
-        sweep(2, (2, 3, 1, 0))
-
-        s = PAIRS[1]
-        sort_words(s, 0)
-        turn_blocks(s, 0)
-        sort_words(s, 1)
-        pair_words(s, 0)
-        turn_blocks(s, 1)
-        add_bias(1)
-        sort_words(s, 2)
-        pair_words(s, 1)
-        turn_blocks(s, 2)
-        add_bias(0)
-        sort_words(s, 3)
-        pair_words(s, 2)
-        turn_blocks(s, 3)
-        pair_words(s, 3)
-        quantise_of_pair(s, 0)
-        quantise_of_pair(s, 1)
-        tanh_store(1)
-        tanh_store(0)
-
-        pair(2, 0)
-        pair(3, 1)
+        pair(7, 1)
         open_slab(4, [2])
-        pair(4, 2)
-        add_bias(2)
-        tanh_store(2)
-        pair(3, 0)
         pair(4, 1)
-        open_slab(SPLIT, [3, 7])
+        pair(4, 2)
+        open_slab(SPLIT, [3, 6])
         pair(SPLIT, 2, 0)
         pair(SPLIT, 2, 1)
-        add_bias(3)
-        tanh_store(3)
         pair(4, 0)
-        pair(SPLIT, 1, 0)
-        pair(SPLIT, 1, 1)
-        pair(6, 2)
         add_bias(4)
         tanh_store(4)
+        pair(6, 2)
+        pair(SPLIT, 1, 0)
+        pair(SPLIT, 1, 1)
         pair(7, 2)
         add_bias(7)
         tanh_store(7)

@@ -85,7 +85,7 @@ def tile_predictor_pa_e_kernel(tc, x, W1_words, W1_scales, b1, out):
 
         def load_pair(s):
             for b in range(4):
-                for a in range(4):
+                for a in (0, 2, 1, 3):
                     nc.sync.dma_start(
                         out=x_pair[s][32 * a : 32 * a + 32, b, :].rearrange("p (m w) -> p m w", m=2 * GROUPS),
                         in_=x_by_block[b][a][:, GROUPS * s : GROUPS * (s + 2), :],
@@ -120,7 +120,7 @@ def tile_predictor_pa_e_kernel(tc, x, W1_words, W1_scales, b1, out):
             words = x_sb[s][:].bitcast(F32)
             grouped = new_grouped(s)
             for half in range(GROUPS // 2):
-                bank = bank_tile(2 * (i % 2) + half, [P, 2, 2, P], "turned%d_%d" % (s, half))
+                bank = bank_tile(2 * (i % 4) + half, [P, 2, 2, P], "turned%d_%d" % (s, half))
                 for g in range(2):
                     for u in range(2):
                         group = 2 * half + g

@@ -254,7 +254,8 @@ def tile_predictor_pa_e_kernel(tc, x, W1_words, W1_scales, b1, out):
         open_slab(1, [7])
         open_slab(2, [0])
         open_slab(3, [1])
-        sweep(0, (6, 7, 0, 1, 2, 3))
+        sweep(0, (6, 7, 0, 1))
+        sweep(0, (2, 3))
 
         s = PAIRS[0]
         sort_words(s, 0)

@@ -282,8 +282,6 @@ def tile_predictor_pa_e_kernel(tc, x, W1_words, W1_scales, b1, out):
         add_bias(4)
         tanh_store(4)
         pair(6, 2)
-        pair(SPLIT, 1, 0)
-        pair(SPLIT, 1, 1)
         pair(7, 2)
         add_bias(7)
         tanh_store(7)
@@ -291,6 +289,7 @@ def tile_predictor_pa_e_kernel(tc, x, W1_words, W1_scales, b1, out):
         add_bias(6)
         tanh_store(6)
         for i in range(2):
+            pair(SPLIT, 1, i)
             pair(SPLIT, 0, i)
             add_bias(SPLIT, i)
             tanh_store(SPLIT, i)

@@ -91,22 +91,29 @@ def tile_predictor_pa_e_kernel(tc, x, W1_words, W1_scales, b1, out):
                         in_=x_by_block[b][a][:, GROUPS * s : GROUPS * (s + 2), :],
                     )
 
-        def load_w(tap):
+        def load_w_scales(tap):
             groups = slice(GROUPS * tap, GROUPS * (tap + 1))
             for quadrant in range(4):
                 nc.sync.dma_start(
                     out=w_scales[32 * quadrant : 32 * quadrant + 16, tap, :].bitcast(I32),
                     in_=W1_scales[groups, 4 * quadrant : 4 * quadrant + 4, :].bitcast(I32),
                 )
-            for g in range(GROUPS * tap, GROUPS * (tap + 1)):
+
+        def load_w_codes(tap, groups):
+            for g in groups:
+                g = GROUPS * tap + g
                 nc.sync.dma_start(out=w_codes[g][:].bitcast(I32), in_=w_words_by_group[g].bitcast(I32))
 
         load_x(ON_TENSOR[0], GROUPS)
-        for s in ON_TENSOR[1:]:
+        for s in ON_TENSOR[1:-1]:
             load_x(s, 1)
-        load_w(0)
-        load_w(1)
-        load_w(2)
+        load_w_scales(0)
+        load_w_codes(0, range(0, 1))
+        load_x(ON_TENSOR[-1], 1)
+        load_w_codes(0, range(1, GROUPS))
+        for tap in range(1, TAPS):
+            load_w_scales(tap)
+            load_w_codes(tap, range(GROUPS))
         nc.sync.dma_start(out=bias[:], in_=b1[0].partition_broadcast(P))
         load_pair(PAIRS[0])
 
@@ -241,6 +248,13 @@ def tile_predictor_pa_e_kernel(tc, x, W1_words, W1_scales, b1, out):
             nc.sync.dma_start(out=out_by_slab[o][:, n_cols], in_=result[:, 0:width])
 
         for i in range(len(ON_TENSOR)):
+            if i == len(ON_TENSOR) - 1:
+                open_slab(6, [4])
+                open_slab(7, [5])
+                open_slab(0, [6])
+                open_slab(1, [7])
+                for o in (6, 7, 0, 1):
+                    mx_pass(o, 0, 0, 0)
             transpose_slab(i, ON_TENSOR[i])
             if i > 0:
                 quantise_position(ON_TENSOR[i - 1] + WRAP, grouped_of[ON_TENSOR[i - 1]][:])
@@ -248,13 +262,11 @@ def tile_predictor_pa_e_kernel(tc, x, W1_words, W1_scales, b1, out):
         for c in (1, 0):
             quantise_position(c, move_on_one_column(grouped_of[SLABS - WRAP + c], "moved%d" % c))
 
-        open_slab(6, [4])
-        open_slab(7, [5])
-        open_slab(0, [6])
-        open_slab(1, [7])
         open_slab(2, [0])
         open_slab(3, [1])
-        sweep(0, (6, 7, 0, 1))
+        for g in range(1, GROUPS):
+            for o in (6, 7, 0, 1):
+                mx_pass(o, 0, 0, g)
         sweep(0, (2, 3))
 
         s = PAIRS[0]

@@ -54,19 +54,23 @@ def tile_predictor_pa_e_kernel(tc, x, W1_words, W1_scales, b1, out):
         for s in PAIRS:
             x_pair[s] = keep.tile([P, 4, 2 * K_PASS], BF16, name="x_pair%d" % s)
             grouped_pair[s] = keep.tile([P, 2, GROUPS, P, PACK], BF16, name="grouped_pair%d" % s, align_bytes=64)
+        XS_PAD = 64
+        WC_PAD = 32
         x_codes = [
-            keep.tile([P, GROUPS * P], U32, name="x_codes%d" % c, align_bytes=64)
+            keep.tile([P, GROUPS * P], U32, name="x_codes%d" % c, align_bytes=256)
             for c in range(POSITIONS)
         ]
-        x_scales = [
-            keep.tile([P, GROUPS * P], U8, name="x_scales%d" % c, align_bytes=64)
+        x_scales_padded = [
+            keep.tile([P, XS_PAD + GROUPS * P], U8, name="x_scales%d" % c, align_bytes=256)
             for c in range(POSITIONS)
         ]
-        w_codes = [
-            keep.tile([P, C], U32, name="w_codes%d" % g, align_bytes=64)
+        x_scales = [t[:, XS_PAD : XS_PAD + GROUPS * P] for t in x_scales_padded]
+        w_codes_padded = [
+            keep.tile([P, WC_PAD + C], U32, name="w_codes%d" % g, align_bytes=256)
             for g in range(TAPS * GROUPS)
         ]
-        w_scales = keep.tile([P, TAPS, C], U8, align_bytes=64)
+        w_codes = [t[:, WC_PAD : WC_PAD + C] for t in w_codes_padded]
+        w_scales = keep.tile([P, TAPS, C], U8, align_bytes=256)
         identity = keep.tile([P, P], F32)
         bias = keep.tile([P, C], BF16)
         counts = keep.tile([P, SLABS], F32)
@@ -102,7 +106,7 @@ def tile_predictor_pa_e_kernel(tc, x, W1_words, W1_scales, b1, out):
         def load_w_codes(tap, groups):
             for g in groups:
                 g = GROUPS * tap + g
-                nc.sync.dma_start(out=w_codes[g][:].bitcast(I32), in_=w_words_by_group[g].bitcast(I32))
+                nc.sync.dma_start(out=w_codes[g].bitcast(I32), in_=w_words_by_group[g].bitcast(I32))
 
         load_x(ON_TENSOR[0], GROUPS)
         for s in ON_TENSOR[1:-1]:
@@ -146,7 +150,7 @@ def tile_predictor_pa_e_kernel(tc, x, W1_words, W1_scales, b1, out):
         def quantise_position(c, grouped):
             nc.vector.quantize_mx(
                 out=x_codes[c][:].bitcast(FP8X4),
-                scales=x_scales[c][:],
+                scales=x_scales[c],
                 in_=grouped.rearrange("p g j t -> p (g j t)"),
             )
 

@@ -108,12 +108,12 @@ def tile_predictor_pa_e_kernel(tc, x, W1_words, W1_scales, b1, out):
                 g = GROUPS * tap + g
                 nc.sync.dma_start(out=w_codes[g].bitcast(I32), in_=w_words_by_group[g].bitcast(I32))
 
-        load_x(ON_TENSOR[0], GROUPS)
-        for s in ON_TENSOR[1:-1]:
-            load_x(s, 1)
+        PIECES = (1, 1, 1, 1, 1, 1)
+        for i in range(len(ON_TENSOR) - 1):
+            load_x(ON_TENSOR[i], PIECES[i])
         load_w_scales(0)
         load_w_codes(0, range(0, 1))
-        load_x(ON_TENSOR[-1], 1)
+        load_x(ON_TENSOR[-1], PIECES[-1])
         load_w_codes(0, range(1, GROUPS))
         for tap in range(1, TAPS):
             load_w_scales(tap)

@@ -111,7 +111,8 @@ def tile_predictor_pa_e_kernel(tc, x, W1_words, W1_scales, b1, out):
         PIECES = (1, 1, 1, 1, 1, 1)
         for i in range(len(ON_TENSOR) - 1):
             load_x(ON_TENSOR[i], PIECES[i])
-        load_w_scales(0)
+            if i == 1:
+                load_w_scales(0)
         load_w_codes(0, range(0, 1))
         load_x(ON_TENSOR[-1], PIECES[-1])
         load_w_codes(0, range(1, GROUPS))

from contextlib import ExitStack

import concourse.mybir as mybir
from concourse.masks import make_identity

F32 = mybir.dt.float32
BF16 = mybir.dt.bfloat16
I32 = mybir.dt.int32
U32 = mybir.dt.uint32
U8 = mybir.dt.uint8
FP8X4 = mybir.dt.float8_e4m3fn_x4

P = 128
PACK = 4
K_PASS = P * PACK

ROWS, E, C, TAPS = 1024, 2048, 512, 3
GROUPS = E // K_PASS
SLABS = ROWS // P
WRAP = TAPS - 1
POSITIONS = SLABS + WRAP
F32_WORDS = K_PASS // 2

FLOPS = 2 * ROWS * TAPS * E * C


def tile_predictor_pa_e_kernel(tc, x, W1_words, W1_scales, b1, out):
    nc = tc.nc
    x_by_slab = x.rearrange("(j s) k -> s j k", s=SLABS)
    x_by_block = x.rearrange("(b beta s) k -> b beta (s k)", s=SLABS, beta=32).rearrange(
        "b beta (m a w) -> b a beta m w", a=4, w=P
    )
    out_by_slab = out.rearrange("(j s) c -> s j c", s=SLABS)
    w_words_by_group = W1_words.rearrange("g p n t -> g p (n t)")
    HALF = C // 2
    ON_TENSOR = (6, 7, 0, 1, 2, 3)
    PAIRS = (4,)
    SPLIT = 5

    with ExitStack() as ctx:
        ctx.enter_context(tc.manual_schedule())
        keep = ctx.enter_context(tc.tile_pool(name="keep", bufs=1))
        stage = ctx.enter_context(tc.tile_pool(name="stage", bufs=4))
        psum = ctx.enter_context(tc.psum_pool(name="psum", bufs=1))

        def bank_tile(b, shape, name):
            return psum.tile(shape, F32, tag="bank%d" % b, name=name)

        x_sb = {}
        for s in ON_TENSOR:
            x_sb[s] = keep.tile([P, E], BF16, name="x_sb%d" % s)
        x_pair = {}
        grouped_pair = {}
        for s in PAIRS:
            x_pair[s] = keep.tile([P, 4, 2 * K_PASS], BF16, name="x_pair%d" % s)
            grouped_pair[s] = keep.tile([P, 2, GROUPS, P, PACK], BF16, name="grouped_pair%d" % s, align_bytes=64)
        XS_PAD = 64
        WC_PAD = 32
        x_codes = [
            keep.tile([P, GROUPS * P], U32, name="x_codes%d" % c, align_bytes=256)
            for c in range(POSITIONS)
        ]
        x_scales_padded = [
            keep.tile([P, XS_PAD + GROUPS * P], U8, name="x_scales%d" % c, align_bytes=256)
            for c in range(POSITIONS)
        ]
        x_scales = [t[:, XS_PAD : XS_PAD + GROUPS * P] for t in x_scales_padded]
        w_codes_padded = [
            keep.tile([P, WC_PAD + C], U32, name="w_codes%d" % g, align_bytes=256)
            for g in range(TAPS * GROUPS)
        ]
        w_codes = [t[:, WC_PAD : WC_PAD + C] for t in w_codes_padded]
        w_scales = keep.tile([P, TAPS, C], U8, align_bytes=256)
        identity = keep.tile([P, P], F32)
        bias = keep.tile([P, C], BF16)
        counts = keep.tile([P, SLABS], F32)

        nc.vector.memset(w_scales[:].bitcast(I32), 0)
        make_identity(nc, identity[:])
        nc.vector.memset(counts[:], float(TAPS))
        for row in range(WRAP):
            nc.vector.memset(counts[0:1, row : row + 1], float(row + 1))

        def load_x(s, pieces):
            width = E // pieces
            for piece in range(pieces):
                cols = slice(width * piece, width * (piece + 1))
                nc.sync.dma_start(out=x_sb[s][:, cols], in_=x_by_slab[s][:, cols])

        def load_pair(s):
            for b in range(4):
                for a in (0, 2, 1, 3):
                    nc.sync.dma_start(
                        out=x_pair[s][32 * a : 32 * a + 32, b, :].rearrange("p (m w) -> p m w", m=2 * GROUPS),
                        in_=x_by_block[b][a][:, GROUPS * s : GROUPS * (s + 2), :],
                    )

        def load_w_scales(tap):
            groups = slice(GROUPS * tap, GROUPS * (tap + 1))
            for quadrant in range(4):
                nc.sync.dma_start(
                    out=w_scales[32 * quadrant : 32 * quadrant + 16, tap, :].bitcast(I32),
                    in_=W1_scales[groups, 4 * quadrant : 4 * quadrant + 4, :].bitcast(I32),
                )

        def load_w_codes(tap, groups):
            for g in groups:
                g = GROUPS * tap + g
                nc.sync.dma_start(out=w_codes[g].bitcast(I32), in_=w_words_by_group[g].bitcast(I32))

        PIECES = (1, 1, 1, 1, 1, 1)
        for i in range(len(ON_TENSOR) - 1):
            load_x(ON_TENSOR[i], PIECES[i])
            if i == 1:
                load_w_scales(0)
        load_w_codes(0, range(0, 1))
        load_x(ON_TENSOR[-1], PIECES[-1])
        load_w_codes(0, range(1, GROUPS))
        for tap in range(1, TAPS):
            load_w_scales(tap)
            load_w_codes(tap, range(GROUPS))
        nc.sync.dma_start(out=bias[:], in_=b1[0].partition_broadcast(P))
        load_pair(PAIRS[0])

        grouped_of = {}

        def new_grouped(s):
            grouped_of[s] = keep.tile([P, GROUPS, P, PACK], BF16, align_bytes=64, name="grouped%d" % s)
            return grouped_of[s]

        def transpose_slab(i, s):
            words = x_sb[s][:].bitcast(F32)
            grouped = new_grouped(s)
            for half in range(GROUPS // 2):
                bank = bank_tile(2 * (i % 4) + half, [P, 2, 2, P], "turned%d_%d" % (s, half))
                for g in range(2):
                    for u in range(2):
                        group = 2 * half + g
                        nc.tensor.transpose(
                            bank[:, g, u, :],
                            words[:, F32_WORDS * group + u : F32_WORDS * (group + 1) : 2],
                            identity[:],
                        )
                dst = grouped[:, 2 * half : 2 * half + 2].bitcast(F32)
                src = bank[:].rearrange("p g u j -> p g j u")
                if half == 1 and i % 2 == 1:
                    nc.vector.tensor_copy(out=dst, in_=src)
                else:
                    nc.scalar.copy(out=dst, in_=src)

        def quantise_position(c, grouped):
            nc.vector.quantize_mx(
                out=x_codes[c][:].bitcast(FP8X4),
                scales=x_scales[c],
                in_=grouped.rearrange("p g j t -> p (g j t)"),
            )

        def move_on_one_column(grouped, name):
            moved = stage.tile([P, GROUPS, P, PACK], BF16, align_bytes=64, name=name, tag="moved")
            nc.vector.memset(moved[:, :, 0, :].bitcast(F32), 0.0)
            nc.vector.tensor_copy(
                out=moved[:, :, 1:P, :].bitcast(F32), in_=grouped[:, :, 0 : P - 1, :].bitcast(F32)
            )
            return moved[:]

        sorted_of = {}
        turned_of = {}
        QUARTER = 2 * F32_WORDS

        def sort_words(s, b):
            sorted_of[(s, b)] = stage.tile([P, QUARTER], F32, align_bytes=64, name="sorted%d_%d" % (s, b), tag="sorted")
            nc.scalar.copy(
                out=sorted_of[(s, b)][:].rearrange("p (u m i) -> p u m i", u=2, i=32),
                in_=x_pair[s][:, b, :].bitcast(F32).rearrange("p (m i u) -> p u m i", u=2, i=32),
            )

        def turn_blocks(s, b):
            turned_of[(s, b)] = stage.tile([P, QUARTER], F32, align_bytes=64, name="turnedv%d_%d" % (s, b), tag="turnedv")
            nc.vector.transpose(out=turned_of[(s, b)][:], in_=sorted_of[(s, b)][:])

        def pair_words(s, b):
            nc.scalar.copy(
                out=grouped_pair[s][:].bitcast(F32).rearrange("p s g j u -> p (s g) j u")[:, :, 32 * b : 32 * (b + 1), :],
                in_=turned_of[(s, b)][:].rearrange("p (u m beta) -> p m beta u", u=2, beta=32),
            )

        def quantise_of_pair(s, k):
            quantise_position(s + k + WRAP, grouped_pair[s][:, k])

        halves = [slice(HALF * h, HALF * (h + 1)) for h in range(2)]
        whole = slice(0, C)
        parts_of = {}
        passes_done = {}

        def open_slab(o, banks):
            if len(banks) == 1:
                parts_of[o] = [(bank_tile(banks[0], [P, C], "acc%d" % o), whole)]
            else:
                parts_of[o] = [
                    (bank_tile(banks[h], [P, HALF], "acc%d_%d" % (o, h)), halves[h]) for h in range(2)
                ]
            for i in range(len(banks)):
                passes_done[(o, i)] = 0

        def mx_pass(o, i, tap, g):
            acc_tile, n_cols = parts_of[o][i]
            c = o + WRAP - tap
            cols = slice(P * g, P * (g + 1))
            done = passes_done[(o, i)]
            nc.tensor.matmul_mx(
                out=acc_tile[:],
                lhsT=x_codes[c][:, cols].bitcast(FP8X4),
                lhsT_scale=x_scales[c][:, cols],
                rhs=w_codes[GROUPS * tap + g][:, n_cols].bitcast(FP8X4),
                rhs_scale=w_scales[PACK * g : P, tap, n_cols],
                start=(done == 0),
                stop=(done == TAPS * GROUPS - 1),
            )
            passes_done[(o, i)] = done + 1

        def sweep(tap, outs):
            for g in range(GROUPS):
                for o in outs:
                    mx_pass(o, 0, tap, g)

        def pair(o, tap, i=0):
            for g in range(GROUPS):
                mx_pass(o, i, tap, g)

        biased_of = {}

        def add_bias(o, i=0):
            acc_tile, n_cols = parts_of[o][i]
            biased = stage.tile([P, C], F32, name="biased%d_%d" % (o, i), tag="biased")
            width = n_cols.stop - n_cols.start
            nc.vector.scalar_tensor_tensor(
                out=biased[:, 0:width],
                in0=bias[:, n_cols],
                scalar=counts[:, o : o + 1],
                in1=acc_tile[:],
                op0=mybir.AluOpType.mult,
                op1=mybir.AluOpType.add,
            )
            biased_of[(o, i)] = biased

        def tanh_store(o, i=0):
            n_cols = parts_of[o][i][1]
            width = n_cols.stop - n_cols.start
            result = stage.tile([P, C], F32, name="result%d_%d" % (o, i), tag="result")
            nc.scalar.activation(
                out=result[:, 0:width], in_=biased_of[(o, i)][:, 0:width], func=mybir.ActivationFunctionType.Tanh
            )
            nc.sync.dma_start(out=out_by_slab[o][:, n_cols], in_=result[:, 0:width])

        for i in range(len(ON_TENSOR)):
            if i == len(ON_TENSOR) - 1:
                open_slab(6, [4])
                open_slab(7, [5])
                open_slab(0, [6])
                open_slab(1, [7])
                for o in (6, 7, 0, 1):
                    mx_pass(o, 0, 0, 0)
            transpose_slab(i, ON_TENSOR[i])
            if i > 0:
                quantise_position(ON_TENSOR[i - 1] + WRAP, grouped_of[ON_TENSOR[i - 1]][:])
        quantise_position(ON_TENSOR[-1] + WRAP, grouped_of[ON_TENSOR[-1]][:])
        for c in (1, 0):
            quantise_position(c, move_on_one_column(grouped_of[SLABS - WRAP + c], "moved%d" % c))

        open_slab(2, [0])
        open_slab(3, [1])
        for g in range(1, GROUPS):
            for o in (6, 7, 0, 1):
                mx_pass(o, 0, 0, g)
        sweep(0, (2, 3))

        s = PAIRS[0]
        sort_words(s, 0)
        for o in range(4):
            pair(o, 1)
            pair(o, 2)
            add_bias(o)
            turn_blocks(s, o)
            tanh_store(o)
            if o < 3:
                sort_words(s, o + 1)
            pair_words(s, o)
        quantise_of_pair(s, 0)
        quantise_of_pair(s, 1)

        pair(7, 1)
        open_slab(4, [2])
        pair(4, 1)
        pair(4, 2)
        open_slab(SPLIT, [3, 6])
        pair(SPLIT, 2, 0)
        pair(SPLIT, 2, 1)
        pair(4, 0)
        add_bias(4)
        tanh_store(4)
        pair(6, 2)
        pair(7, 2)
        add_bias(7)
        tanh_store(7)
        pair(6, 1)
        add_bias(6)
        tanh_store(6)
        for i in range(2):
            pair(SPLIT, 1, i)
            pair(SPLIT, 0, i)
            add_bias(SPLIT, i)
            tanh_store(SPLIT, i)
